import numpy as np
import ml_dtypes


def mxq(x, axis, fmt="e4m3"):
    dtype, down = {"e4m3": (ml_dtypes.float8_e4m3fn, 7), "e5m2": (ml_dtypes.float8_e5m2, 14)}[fmt]
    v = np.moveaxis(np.asarray(x, np.float32).astype(ml_dtypes.bfloat16).astype(np.float64), axis, -1)
    blocks = v.reshape(v.shape[:-1] + (-1, 32))
    amax = np.abs(blocks).max(-1, keepdims=True)
    byte = np.maximum(np.where(amax > 0, np.frexp(amax)[1] - 1 + 127, 0) - down, 1)
    scale = np.exp2(byte - 127.0)
    codes = (blocks / scale).astype(np.float32).astype(dtype).astype(np.float64)
    return np.moveaxis((codes * scale).reshape(v.shape), -1, axis)


WIDE = False


def mx_kscale(k):
    if not WIDE:
        return np.ones(k)
    levels = np.array([10, -10, 5, -5, 0])
    a = np.random.permutation(np.resize(levels, k // 512 * 4)).reshape(k // 512, 4)
    idx = np.arange(k)
    return np.exp2(a[idx // 512, idx % 128 // 32])


BF16 = ml_dtypes.bfloat16


def bf(x):
    return np.asarray(x, np.float32).astype(BF16)


def f64(x):
    return np.asarray(x).astype(np.float64)


B, N, NIN, CTX, H, NOUT = 8, 512, 512, 3, 512, 2
F = NIN * CTX


def shift_down(y, d):
    return np.pad(y[:, :-d, :], ((0, 0), (d, 0), (0, 0)))


def shift_up(y, d):
    return np.pad(y[:, d:, :], ((0, 0), (0, d), (0, 0)))


def context_linear(xq, w, shifts):
    y = xq @ mxq(w[:, :NIN].T, 0, "e4m3")
    c = 1
    for d in range(1, CTX // 2 + 1):
        for shift in shifts:
            y = y + shift(xq @ mxq(w[:, c * NIN:(c + 1) * NIN].T, 0, "e4m3"), d)
            c += 1
    return y


def setup_inputs():
    s, u = mx_kscale(NIN), mx_kscale(H)
    return {"t_bil": bf(np.random.standard_normal((B, N, NOUT, H)) * 0.15 / u),
            "x_r": bf(np.random.standard_normal((B, N, NIN)) * s),
            "W_r": bf(np.random.standard_normal((H, F)) / np.sqrt(F) / np.tile(s, CTX) * u[:, None]),
            "b_r": bf(np.random.standard_normal(H) * 0.3 * u),
            "b_bil": bf(np.random.standard_normal(NOUT))}


def reference(t_bil, x_r, W_r, b_r, b_bil):
    xq = mxq(f64(x_r), 2, "e4m3")
    hr = np.maximum(context_linear(xq, f64(W_r), (shift_up, shift_down)) + f64(b_r), 0.0)
    tq = mxq(f64(t_bil).reshape(B, N * NOUT, H), 2, "e4m3")
    sc = tq @ mxq(hr.transpose(0, 2, 1), 1, "e4m3")
    return sc.reshape(B, N, NOUT, N).transpose(0, 1, 3, 2) + f64(b_bil)

@@ -1,0 +1,204 @@
+from contextlib import ExitStack
+
+import concourse.bass as bass
+import concourse.masks as masks
+import concourse.mybir as mybir
+import concourse.tile as tile
+
+F32 = mybir.dt.float32
+BF16 = mybir.dt.bfloat16
+U32 = mybir.dt.uint32
+U8 = mybir.dt.uint8
+FP8X4 = mybir.dt.float8_e4m3fn_x4
+ACT = mybir.ActivationFunctionType
+ALU = mybir.AluOpType
+
+P = 128
+B = 8
+FLOPS = 2 * 8 * 512 * 512 * 1536 + 2 * 8 * 1024 * 512 * 512
+
+NT = 6
+NB = 2
+NO = 4
+MANUAL = False
+
+
+def tile_bilinearpairedlayer_pb_t_kernel(tc, t_bil, x_r, W_r, b_r, b_bil, out):
+    nc = tc.nc
+    with ExitStack() as ctx:
+        sb = ctx.enter_context(tc.tile_pool(name="sb", bufs=1))
+        ps = ctx.enter_context(tc.psum_pool(name="ps", bufs=1))
+
+        ident = sb.tile([P, P], F32, name="ident")
+        x_sb = [sb.tile([P, 2048], BF16, name="x%d" % i) for i in range(B)]
+        t_sb = [sb.tile([P, 4096], BF16, name="t%d" % i) for i in range(NT)]
+        w_sb = sb.tile([P, 6144], BF16, name="w_sb")
+        wg = sb.tile([P, 6144], BF16, name="wg", align_bytes=64)
+        wc = sb.tile([P, 1536], U32, name="wc", align_bytes=64)
+        ws = sb.tile([P, 1536], U8, name="ws", align_bytes=64)
+        xg = [sb.tile([P, 3072], BF16, name="xg%d" % i, align_bytes=64) for i in range(NB)]
+        xc = [sb.tile([P, 768], U32, name="xc%d" % i, align_bytes=64) for i in range(NB)]
+        xs = [sb.tile([P, 768], U8, name="xs%d" % i, align_bytes=64) for i in range(NB)]
+        tg = [sb.tile([P, 4096], BF16, name="tg%d" % i, align_bytes=64) for i in range(NB)]
+        tcd = [sb.tile([P, 1024], U32, name="tcd%d" % i, align_bytes=64) for i in range(NB)]
+        tsc = [sb.tile([P, 1024], U8, name="tsc%d" % i, align_bytes=64) for i in range(NB)]
+        hrt = [sb.tile([P, 2048], BF16, name="hrt%d" % i) for i in range(NB)]
+        hg = [sb.tile([P, 2048], BF16, name="hg%d" % i, align_bytes=64) for i in range(NB)]
+        hc = [sb.tile([P, 512], U32, name="hc%d" % i, align_bytes=64) for i in range(NB)]
+        hs = [sb.tile([P, 512], U8, name="hs%d" % i, align_bytes=64) for i in range(NB)]
+        o_sb = [sb.tile([P, 2048], F32, name="o%d" % i) for i in range(NO)]
+        br_bf = sb.tile([P, 4], BF16, name="br_bf")
+        br = sb.tile([P, 4], F32, name="br")
+        bb_bf = sb.tile([P, 2], BF16, name="bb_bf")
+        bbt = sb.tile([P, 512], F32, name="bbt")
+
+        pt = [ps.tile([P, 512], F32, name="pt%d" % i) for i in range(3)]
+        p1 = [ps.tile([P, 512], F32, name="p1_%d" % i) for i in range(2)]
+        p2 = [ps.tile([P, 512], F32, name="p2_%d" % i) for i in range(3)]
+        cnt = {"pt": 0, "p1": 0, "p2": 0, "o": 0}
+
+        if MANUAL:
+            ctx.enter_context(tc.manual_schedule())
+
+        def load_x(b):
+            nc.sync.dma_start(out=x_sb[b][:], in_=x_r[b].rearrange("(p a) f -> p (a f)", a=4))
+
+        def load_t(b):
+            nc.sync.dma_start(out=t_sb[b % NT][:], in_=t_bil[b].rearrange("(p a) k g -> p (a k g)", a=4))
+
+        w_view = W_r.rearrange("(u p e) f -> p u (e f)", u=2, e=2)
+        load_x(0)
+        for u in range(2):
+            nc.sync.dma_start(out=w_sb[:, u * 3072:(u + 1) * 3072], in_=w_view[:, u, :])
+        with nc.allow_non_contiguous_dma(reason="two small bias vectors"):
+            nc.scalar.dma_start(out=br_bf[:].rearrange("p (u e) -> p u e", u=2),
+                                in_=b_r.rearrange("(u p e) -> p u e", u=2, e=2))
+            nc.scalar.dma_start(out=bb_bf[:], in_=b_bil.partition_broadcast(P))
+        load_t(0)
+        for b in range(1, B):
+            load_x(b)
+            if b < NT:
+                load_t(b)
+
+        masks.make_identity(nc, ident[:])
+        for i in range(NB):
+            nc.vector.memset(xg[i][:, 0:4], 0.0)
+            nc.vector.memset(xg[i][:, 3068:3072], 0.0)
+        nc.vector.tensor_copy(out=br[:], in_=br_bf[:])
+        nc.vector.tensor_copy(out=bbt[:].rearrange("p (j k) -> p j k", k=2),
+                              in_=bb_bf[:].unsqueeze(1).to_broadcast([P, 256, 2]))
+
+        def flip(src, dst, m, dst_off, eng):
+            bank = pt[cnt["pt"] % 3]
+            cnt["pt"] += 1
+            s32 = src[:].bitcast(F32)
+            for i in range(4):
+                c0 = 512 * m + 128 * i
+                nc.tensor.transpose(bank[:, 128 * i:128 * (i + 1)], s32[:, c0:c0 + 128], ident[:])
+            o_ap = dst[:].bitcast(F32)[:, dst_off:dst_off + 512].rearrange("p (a c u) -> p a c u", a=2, u=2)
+            i_ap = bank[:].rearrange("p (a u c) -> p a c u", a=2, u=2)
+            if eng == "s":
+                nc.scalar.copy(out=o_ap, in_=i_ap)
+            else:
+                nc.vector.tensor_copy(out=o_ap, in_=i_ap)
+
+        def quant(codes, scales, src, c0, width):
+            nc.vector.quantize_mx(out=codes[:, c0 // 4:(c0 + width) // 4].bitcast(FP8X4),
+                                  scales=scales[:, c0 // 4:(c0 + width) // 4],
+                                  in_=src[:, c0:c0 + width])
+
+        def tx(b):
+            for m in range(2):
+                flip(x_sb[b], xg[b % NB], m, 256 + 512 * m, "s")
+
+        def qx(b):
+            g = xg[b % NB]
+            nc.vector.tensor_copy(out=g[:, 2560:3068], in_=g[:, 516:1024])
+            nc.vector.tensor_copy(out=g[:, 4:512], in_=g[:, 2048:2556])
+            quant(xc[b % NB], xs[b % NB], g, 0, 2048)
+            quant(xc[b % NB], xs[b % NB], g, 2048, 1024)
+
+        def tt(b):
+            for m in range(4):
+                flip(t_sb[b % NT], tg[b % NB], m, 512 * m, "s")
+
+        def qt(b):
+            quant(tcd[b % NB], tsc[b % NB], tg[b % NB], 0, 4096)
+
+        def s1(b, t):
+            bank = p1[cnt["p1"] % 2]
+            cnt["p1"] += 1
+            for w, off in ((0, 128), (1, 256), (2, 0)):
+                s = t * 3 + w
+                nc.tensor.matmul_mx(out=bank[:],
+                                    lhsT=wc[:, s * 128:(s + 1) * 128].bitcast(FP8X4),
+                                    lhsT_scale=ws[:, s * 128:(s + 1) * 128],
+                                    rhs=xc[b % NB][:, off:off + 512].bitcast(FP8X4),
+                                    rhs_scale=xs[b % NB][:, off:off + 512],
+                                    start=(w == 0), stop=(w == 2))
+            nc.scalar.activation(out=hrt[b % NB][:, t * 512:(t + 1) * 512].rearrange("p (q a) -> p q a", a=4),
+                                 in_=bank[:].rearrange("p (a q) -> p q a", a=4),
+                                 func=ACT.Relu, bias=br[:, t:t + 1], scale=1.0)
+
+        def qh(b):
+            nc.vector.tensor_copy(out=hg[b % NB][:].rearrange("p (c i t) -> p c t i", i=4, t=4),
+                                  in_=hrt[b % NB][:].rearrange("p (t c i) -> p c t i", t=4, i=4))
+            quant(hc[b % NB], hs[b % NB], hg[b % NB], 0, 2048)
+
+        def s2(b, a):
+            if a % 2 == 0:
+                cnt["o"] += 1
+            o = o_sb[(cnt["o"] - 1) % NO]
+            for jh in range(2):
+                bank = p2[cnt["p2"] % 3]
+                cnt["p2"] += 1
+                for k in range(2):
+                    s = 2 * a + k
+                    nc.tensor.matmul_mx(out=bank[:, k * 256:(k + 1) * 256],
+                                        lhsT=tcd[b % NB][:, s * 128:(s + 1) * 128].bitcast(FP8X4),
+                                        lhsT_scale=tsc[b % NB][:, s * 128:(s + 1) * 128],
+                                        rhs=hc[b % NB][:, jh * 256:(jh + 1) * 256].bitcast(FP8X4),
+                                        rhs_scale=hs[b % NB][:, jh * 256:(jh + 1) * 256],
+                                        start=True, stop=True)
+                c0 = (a % 2) * 1024 + jh * 512
+                nc.vector.tensor_tensor(out=o[:, c0:c0 + 512].rearrange("p (j k) -> p j k", k=2),
+                                        in0=bank[:].rearrange("p (k j) -> p j k", k=2),
+                                        in1=bbt[:].rearrange("p (j k) -> p j k", k=2),
+                                        op=ALU.add)
+            if a % 2 == 1:
+                nc.sync.dma_start(out=out[b].rearrange("(p a) j k -> p a (j k)", a=4)[:, a - 1:a + 1, :],
+                                  in_=o[:].rearrange("p (a r) -> p a r", a=2))
+
+        tx(0)
+        for m in range(6):
+            flip(w_sb, wg, m, 512 * m, "v" if m % 2 else "s")
+        qx(0)
+        quant(wc, ws, wg, 0, 2048)
+        quant(wc, ws, wg, 2048, 4096)
+        for n in range(B + 1):
+            if n + 1 < B:
+                tx(n + 1)
+            if n < B:
+                tt(n)
+                if n + NT < B:
+                    load_t(n + NT)
+            if n >= 1:
+                qh(n - 1)
+            if n + 1 < B:
+                qx(n + 1)
+            if n < B:
+                qt(n)
+            if n < B:
+                s1(n, 0)
+                s1(n, 1)
+            if n >= 1:
+                s2(n - 1, 0)
+            if n < B:
+                s1(n, 2)
+            if n >= 1:
+                s2(n - 1, 1)
+            if n < B:
+                s1(n, 3)
+            if n >= 1:
+                s2(n - 1, 2)
+                s2(n - 1, 3)

@@ -1,9 +1,7 @@
 from contextlib import ExitStack
 
-import concourse.bass as bass
 import concourse.masks as masks
 import concourse.mybir as mybir
-import concourse.tile as tile
 
 F32 = mybir.dt.float32
 BF16 = mybir.dt.bfloat16
@@ -17,10 +15,14 @@ P = 128
 B = 8
 FLOPS = 2 * 8 * 512 * 512 * 1536 + 2 * 8 * 1024 * 512 * 512
 
+MANUAL = True
+LAG = 6
+PLAN = (0, 2, 2, 2)
+AHEAD = 2
+RG = ("s",)
+HALO = "v"
+QDELAY = 1
 NT = 6
-NB = 2
-NO = 4
-MANUAL = False
 
 
 def tile_bilinearpairedlayer_pb_t_kernel(tc, t_bil, x_r, W_r, b_r, b_bil, out):
@@ -36,17 +38,17 @@ def tile_bilinearpairedlayer_pb_t_kernel(tc, t_bil, x_r, W_r, b_r, b_bil, out):
         wg = sb.tile([P, 6144], BF16, name="wg", align_bytes=64)
         wc = sb.tile([P, 1536], U32, name="wc", align_bytes=64)
         ws = sb.tile([P, 1536], U8, name="ws", align_bytes=64)
-        xg = [sb.tile([P, 3072], BF16, name="xg%d" % i, align_bytes=64) for i in range(NB)]
-        xc = [sb.tile([P, 768], U32, name="xc%d" % i, align_bytes=64) for i in range(NB)]
-        xs = [sb.tile([P, 768], U8, name="xs%d" % i, align_bytes=64) for i in range(NB)]
-        tg = [sb.tile([P, 4096], BF16, name="tg%d" % i, align_bytes=64) for i in range(NB)]
-        tcd = [sb.tile([P, 1024], U32, name="tcd%d" % i, align_bytes=64) for i in range(NB)]
-        tsc = [sb.tile([P, 1024], U8, name="tsc%d" % i, align_bytes=64) for i in range(NB)]
-        hrt = [sb.tile([P, 2048], BF16, name="hrt%d" % i) for i in range(NB)]
-        hg = [sb.tile([P, 2048], BF16, name="hg%d" % i, align_bytes=64) for i in range(NB)]
-        hc = [sb.tile([P, 512], U32, name="hc%d" % i, align_bytes=64) for i in range(NB)]
-        hs = [sb.tile([P, 512], U8, name="hs%d" % i, align_bytes=64) for i in range(NB)]
-        o_sb = [sb.tile([P, 2048], F32, name="o%d" % i) for i in range(NO)]
+        xg = [sb.tile([P, 3072], BF16, name="xg%d" % i, align_bytes=64) for i in range(2)]
+        xc = [sb.tile([P, 768], U32, name="xc%d" % i, align_bytes=64) for i in range(3)]
+        xs = [sb.tile([P, 768], U8, name="xs%d" % i, align_bytes=64) for i in range(3)]
+        tg = [sb.tile([P, 2048], BF16, name="tg%d" % i, align_bytes=64) for i in range(4)]
+        tcd = [sb.tile([P, 1024], U32, name="tcd%d" % i, align_bytes=64) for i in range(3)]
+        tsc = [sb.tile([P, 1024], U8, name="tsc%d" % i, align_bytes=64) for i in range(3)]
+        hrt = [sb.tile([P, 2048], BF16, name="hrt%d" % i) for i in range(2)]
+        hg = [sb.tile([P, 2048], BF16, name="hg%d" % i, align_bytes=64) for i in range(2)]
+        hc = [sb.tile([P, 512], U32, name="hc%d" % i, align_bytes=64) for i in range(3)]
+        hs = [sb.tile([P, 512], U8, name="hs%d" % i, align_bytes=64) for i in range(3)]
+        o_sb = [sb.tile([P, 2048], F32, name="o%d" % i) for i in range(4)]
         br_bf = sb.tile([P, 4], BF16, name="br_bf")
         br = sb.tile([P, 4], F32, name="br")
         bb_bf = sb.tile([P, 2], BF16, name="bb_bf")
@@ -74,21 +76,22 @@ def tile_bilinearpairedlayer_pb_t_kernel(tc, t_bil, x_r, W_r, b_r, b_bil, out):
             nc.scalar.dma_start(out=br_bf[:].rearrange("p (u e) -> p u e", u=2),
                                 in_=b_r.rearrange("(u p e) -> p u e", u=2, e=2))
             nc.scalar.dma_start(out=bb_bf[:], in_=b_bil.partition_broadcast(P))
-        load_t(0)
-        for b in range(1, B):
-            load_x(b)
+        load_x(1)
+        for b in range(B):
             if b < NT:
                 load_t(b)
+            if b + 2 < B:
+                load_x(b + 2)
 
         masks.make_identity(nc, ident[:])
-        for i in range(NB):
+        for i in range(2):
             nc.vector.memset(xg[i][:, 0:4], 0.0)
             nc.vector.memset(xg[i][:, 3068:3072], 0.0)
         nc.vector.tensor_copy(out=br[:], in_=br_bf[:])
         nc.vector.tensor_copy(out=bbt[:].rearrange("p (j k) -> p j k", k=2),
                               in_=bb_bf[:].unsqueeze(1).to_broadcast([P, 256, 2]))
 
-        def flip(src, dst, m, dst_off, eng):
+        def flip(src, m, dst, dst_off, eng):
             bank = pt[cnt["pt"] % 3]
             cnt["pt"] += 1
             s32 = src[:].bitcast(F32)
@@ -102,28 +105,42 @@ def tile_bilinearpairedlayer_pb_t_kernel(tc, t_bil, x_r, W_r, b_r, b_bil, out):
             else:
                 nc.vector.tensor_copy(out=o_ap, in_=i_ap)
 
-        def quant(codes, scales, src, c0, width):
-            nc.vector.quantize_mx(out=codes[:, c0 // 4:(c0 + width) // 4].bitcast(FP8X4),
-                                  scales=scales[:, c0 // 4:(c0 + width) // 4],
-                                  in_=src[:, c0:c0 + width])
+        def quant(codes, scales, c_off, src, s_off, width):
+            nc.vector.quantize_mx(out=codes[:, c_off:c_off + width // 4].bitcast(FP8X4),
+                                  scales=scales[:, c_off:c_off + width // 4],
+                                  in_=src[:, s_off:s_off + width])
 
-        def tx(b):
-            for m in range(2):
-                flip(x_sb[b], xg[b % NB], m, 256 + 512 * m, "s")
+        def copy_on(eng, o_ap, i_ap):
+            if eng == "v":
+                nc.vector.tensor_copy(out=o_ap, in_=i_ap)
+            elif eng == "s":
+                nc.scalar.copy(out=o_ap, in_=i_ap)
+            else:
+                nc.gpsimd.tensor_scalar(out=o_ap, in0=i_ap, scalar1=1.0, scalar2=0.0, op0=ALU.mult, op1=ALU.add)
 
-        def qx(b):
-            g = xg[b % NB]
-            nc.vector.tensor_copy(out=g[:, 2560:3068], in_=g[:, 516:1024])
-            nc.vector.tensor_copy(out=g[:, 4:512], in_=g[:, 2048:2556])
-            quant(xc[b % NB], xs[b % NB], g, 0, 2048)
-            quant(xc[b % NB], xs[b % NB], g, 2048, 1024)
+        def job(kind, b, m, eng):
+            if kind == "x":
+                flip(x_sb[b], m, xg[b % 2], 256 + 512 * m, eng)
+                return [("x", b, 0)] if m == 1 else []
+            if kind == "w":
+                flip(w_sb, m, wg, 512 * m, eng)
+                return [("w", 0, m // 2)] if m % 2 == 1 else []
+            flip(t_sb[b % NT], m, tg[(2 * b + m // 2) % 4], 512 * (m % 2), eng)
+            if m == 3 and b + NT < B:
+                load_t(b + NT)
+            return [("t", b, m // 2)] if m % 2 == 1 else []
 
-        def tt(b):
-            for m in range(4):
-                flip(t_sb[b % NT], tg[b % NB], m, 512 * m, "s")
-
-        def qt(b):
-            quant(tcd[b % NB], tsc[b % NB], tg[b % NB], 0, 4096)
+        def quantise(kind, b, h):
+            if kind == "x":
+                g = xg[b % 2]
+                copy_on(HALO, g[:, 2560:3068], g[:, 516:1024])
+                copy_on(HALO, g[:, 4:512], g[:, 2048:2556])
+                quant(xc[b % 3], xs[b % 3], 0, g, 0, 2048)
+                quant(xc[b % 3], xs[b % 3], 512, g, 2048, 1024)
+            elif kind == "w":
+                quant(wc, ws, 512 * h, wg, 2048 * h, 2048)
+            else:
+                quant(tcd[b % 3], tsc[b % 3], 512 * h, tg[(2 * b + h) % 4], 0, 2048)
 
         def s1(b, t):
             bank = p1[cnt["p1"] % 2]
@@ -133,72 +150,84 @@ def tile_bilinearpairedlayer_pb_t_kernel(tc, t_bil, x_r, W_r, b_r, b_bil, out):
                 nc.tensor.matmul_mx(out=bank[:],
                                     lhsT=wc[:, s * 128:(s + 1) * 128].bitcast(FP8X4),
                                     lhsT_scale=ws[:, s * 128:(s + 1) * 128],
-                                    rhs=xc[b % NB][:, off:off + 512].bitcast(FP8X4),
-                                    rhs_scale=xs[b % NB][:, off:off + 512],
+                                    rhs=xc[b % 3][:, off:off + 512].bitcast(FP8X4),
+                                    rhs_scale=xs[b % 3][:, off:off + 512],
                                     start=(w == 0), stop=(w == 2))
-            nc.scalar.activation(out=hrt[b % NB][:, t * 512:(t + 1) * 512].rearrange("p (q a) -> p q a", a=4),
+            nc.scalar.activation(out=hrt[b % 2][:, t * 512:(t + 1) * 512].rearrange("p (q a) -> p q a", a=4),
                                  in_=bank[:].rearrange("p (a q) -> p q a", a=4),
                                  func=ACT.Relu, bias=br[:, t:t + 1], scale=1.0)
 
+        def regroup(b):
+            n = len(RG)
+            dst = hg[b % 2][:].rearrange("p (c i t) -> p c t i", i=4, t=4)
+            src = hrt[b % 2][:].rearrange("p (t c i) -> p c t i", t=4, i=4)
+            for i in range(n):
+                c0 = 128 * i // n
+                c1 = 128 * (i + 1) // n
+                copy_on(RG[i], dst[:, c0:c1], src[:, c0:c1])
+
         def qh(b):
-            nc.vector.tensor_copy(out=hg[b % NB][:].rearrange("p (c i t) -> p c t i", i=4, t=4),
-                                  in_=hrt[b % NB][:].rearrange("p (t c i) -> p c t i", t=4, i=4))
-            quant(hc[b % NB], hs[b % NB], hg[b % NB], 0, 2048)
+            quant(hc[b % 3], hs[b % 3], 0, hg[b % 2], 0, 2048)
 
         def s2(b, a):
             if a % 2 == 0:
                 cnt["o"] += 1
-            o = o_sb[(cnt["o"] - 1) % NO]
+            o = o_sb[(cnt["o"] - 1) % 4]
             for jh in range(2):
                 bank = p2[cnt["p2"] % 3]
                 cnt["p2"] += 1
                 for k in range(2):
                     s = 2 * a + k
                     nc.tensor.matmul_mx(out=bank[:, k * 256:(k + 1) * 256],
-                                        lhsT=tcd[b % NB][:, s * 128:(s + 1) * 128].bitcast(FP8X4),
-                                        lhsT_scale=tsc[b % NB][:, s * 128:(s + 1) * 128],
-                                        rhs=hc[b % NB][:, jh * 256:(jh + 1) * 256].bitcast(FP8X4),
-                                        rhs_scale=hs[b % NB][:, jh * 256:(jh + 1) * 256],
+                                        lhsT=tcd[b % 3][:, s * 128:(s + 1) * 128].bitcast(FP8X4),
+                                        lhsT_scale=tsc[b % 3][:, s * 128:(s + 1) * 128],
+                                        rhs=hc[b % 3][:, jh * 256:(jh + 1) * 256].bitcast(FP8X4),
+                                        rhs_scale=hs[b % 3][:, jh * 256:(jh + 1) * 256],
                                         start=True, stop=True)
                 c0 = (a % 2) * 1024 + jh * 512
                 nc.vector.tensor_tensor(out=o[:, c0:c0 + 512].rearrange("p (j k) -> p j k", k=2),
                                         in0=bank[:].rearrange("p (k j) -> p j k", k=2),
                                         in1=bbt[:].rearrange("p (j k) -> p j k", k=2),
                                         op=ALU.add)
-            if a % 2 == 1:
-                nc.sync.dma_start(out=out[b].rearrange("(p a) j k -> p a (j k)", a=4)[:, a - 1:a + 1, :],
-                                  in_=o[:].rearrange("p (a r) -> p a r", a=2))
+            o_view = out[b].rearrange("(p a) j k -> p a (j k)", a=4)
+            if b == B - 1:
+                nc.sync.dma_start(out=o_view[:, a, :], in_=o[:, (a % 2) * 1024:(a % 2 + 1) * 1024])
+            elif a % 2 == 1:
+                nc.sync.dma_start(out=o_view[:, a - 1:a + 1, :], in_=o[:].rearrange("p (a r) -> p a r", a=2))
 
-        tx(0)
-        for m in range(6):
-            flip(w_sb, wg, m, 512 * m, "v" if m % 2 else "s")
-        qx(0)
-        quant(wc, ws, wg, 0, 2048)
-        quant(wc, ws, wg, 2048, 4096)
-        for n in range(B + 1):
-            if n + 1 < B:
-                tx(n + 1)
+        jobs = [("x", 0, 0), ("x", 0, 1)] + [("w", 0, m) for m in range(6)] + [("x", 1, 0), ("x", 1, 1)]
+        for b in range(B):
+            jobs += [("t", b, m) for m in range(4)]
+            if b + 2 < B:
+                jobs += [("x", b + 2, 0), ("x", b + 2, 1)]
+        todo = []
+        for i in range(8 + AHEAD):
+            ready = todo
+            kind, b, m = jobs[i]
+            todo = job(kind, b, m, "v" if i % 2 else "s")
+            for kind, b, h in ready:
+                quantise(kind, b, h)
+        for kind, b, h in todo:
+            quantise(kind, b, h)
+        nxt = 8 + AHEAD
+        waiting = []
+        for tick in range(4 * B + LAG):
+            n = tick // 4
+            q = tick % 4
+            if q == 0 and 1 <= n <= B:
+                regroup(n - 1)
+            for i in range(PLAN[q]):
+                if nxt < len(jobs):
+                    kind, b, m = jobs[nxt]
+                    nxt += 1
+                    waiting += [(tick + QDELAY, item) for item in job(kind, b, m, "s")]
             if n < B:
-                tt(n)
-                if n + NT < B:
-                    load_t(n + NT)
-            if n >= 1:
+                s1(n, q)
+            if tick >= LAG:
+                s2((tick - LAG) // 4, (tick - LAG) % 4)
+            if q == 0 and 1 <= n <= B:
                 qh(n - 1)
-            if n + 1 < B:
-                qx(n + 1)
-            if n < B:
-                qt(n)
-            if n < B:
-                s1(n, 0)
-                s1(n, 1)
-            if n >= 1:
-                s2(n - 1, 0)
-            if n < B:
-                s1(n, 2)
-            if n >= 1:
-                s2(n - 1, 1)
-            if n < B:
-                s1(n, 3)
-            if n >= 1:
-                s2(n - 1, 2)
-                s2(n - 1, 3)
+            for due, item in waiting:
+                if due <= tick:
+                    quantise(item[0], item[1], item[2])
+            waiting = [(due, item) for due, item in waiting if due > tick]

@@ -16,12 +16,13 @@ B = 8
 FLOPS = 2 * 8 * 512 * 512 * 1536 + 2 * 8 * 1024 * 512 * 512
 
 MANUAL = True
-LAG = 6
+LAG = 7
 PLAN = (0, 2, 2, 2)
 AHEAD = 2
-RG = ("s",)
+RG = ("g", "g", "g", "g")
 HALO = "v"
 QDELAY = 1
+QHQ = 1
 NT = 6
 
 
@@ -225,7 +226,7 @@ def tile_bilinearpairedlayer_pb_t_kernel(tc, t_bil, x_r, W_r, b_r, b_bil, out):
                 s1(n, q)
             if tick >= LAG:
                 s2((tick - LAG) // 4, (tick - LAG) % 4)
-            if q == 0 and 1 <= n <= B:
+            if q == QHQ and 1 <= n <= B:
                 qh(n - 1)
             for due, item in waiting:
                 if due <= tick:

@@ -17,7 +17,7 @@ FLOPS = 2 * 8 * 512 * 512 * 1536 + 2 * 8 * 1024 * 512 * 512
 
 MANUAL = True
 LAG = 7
-PLAN = (0, 2, 2, 2)
+PLAN = (0, 3, 0, 3)
 AHEAD = 2
 RG = ("g", "g", "g", "g")
 HALO = "v"
@@ -54,6 +54,7 @@ def tile_bilinearpairedlayer_pb_t_kernel(tc, t_bil, x_r, W_r, b_r, b_bil, out):
         br = sb.tile([P, 4], F32, name="br")
         bb_bf = sb.tile([P, 2], BF16, name="bb_bf")
         bbt = sb.tile([P, 512], F32, name="bbt")
+        warm = sb.tile([P, 2], F32, name="warm")
 
         pt = [ps.tile([P, 512], F32, name="pt%d" % i) for i in range(3)]
         p1 = [ps.tile([P, 512], F32, name="p1_%d" % i) for i in range(2)]
@@ -84,6 +85,8 @@ def tile_bilinearpairedlayer_pb_t_kernel(tc, t_bil, x_r, W_r, b_r, b_bil, out):
             if b + 2 < B:
                 load_x(b + 2)
 
+        nc.vector.memset(warm[:, 0:1], 0.0)
+        nc.scalar.activation(out=warm[:, 1:2], in_=warm[:, 0:1], func=ACT.Relu)
         masks.make_identity(nc, ident[:])
         for i in range(2):
             nc.vector.memset(xg[i][:, 0:4], 0.0)

@@ -16,13 +16,13 @@ B = 8
 FLOPS = 2 * 8 * 512 * 512 * 1536 + 2 * 8 * 1024 * 512 * 512
 
 MANUAL = True
-LAG = 7
-PLAN = (0, 3, 0, 3)
-AHEAD = 2
-RG = ("g", "g", "g", "g")
+LAG = 6
+PLAN = (2, 2, 2, 0)
+AHEAD = 0
+RG = ("g", "g", "g", "s")
 HALO = "v"
 QDELAY = 1
-QHQ = 1
+QHQ = 0
 NT = 6
 
 
@@ -54,7 +54,6 @@ def tile_bilinearpairedlayer_pb_t_kernel(tc, t_bil, x_r, W_r, b_r, b_bil, out):
         br = sb.tile([P, 4], F32, name="br")
         bb_bf = sb.tile([P, 2], BF16, name="bb_bf")
         bbt = sb.tile([P, 512], F32, name="bbt")
-        warm = sb.tile([P, 2], F32, name="warm")
 
         pt = [ps.tile([P, 512], F32, name="pt%d" % i) for i in range(3)]
         p1 = [ps.tile([P, 512], F32, name="p1_%d" % i) for i in range(2)]
@@ -80,13 +79,11 @@ def tile_bilinearpairedlayer_pb_t_kernel(tc, t_bil, x_r, W_r, b_r, b_bil, out):
             nc.scalar.dma_start(out=bb_bf[:], in_=b_bil.partition_broadcast(P))
         load_x(1)
         for b in range(B):
-            if b < NT:
-                load_t(b)
             if b + 2 < B:
                 load_x(b + 2)
+            if b < NT:
+                load_t(b)
 
-        nc.vector.memset(warm[:, 0:1], 0.0)
-        nc.scalar.activation(out=warm[:, 1:2], in_=warm[:, 0:1], func=ACT.Relu)
         masks.make_identity(nc, ident[:])
         for i in range(2):
             nc.vector.memset(xg[i][:, 0:4], 0.0)
@@ -201,9 +198,9 @@ def tile_bilinearpairedlayer_pb_t_kernel(tc, t_bil, x_r, W_r, b_r, b_bil, out):
 
         jobs = [("x", 0, 0), ("x", 0, 1)] + [("w", 0, m) for m in range(6)] + [("x", 1, 0), ("x", 1, 1)]
         for b in range(B):
-            jobs += [("t", b, m) for m in range(4)]
             if b + 2 < B:
                 jobs += [("x", b + 2, 0), ("x", b + 2, 1)]
+            jobs += [("t", b, m) for m in range(4)]
         todo = []
         for i in range(8 + AHEAD):
             ready = todo

@@ -17,7 +17,7 @@ FLOPS = 2 * 8 * 512 * 512 * 1536 + 2 * 8 * 1024 * 512 * 512
 
 MANUAL = True
 LAG = 6
-PLAN = (2, 2, 2, 0)
+PLAN = (3, 0, 3, 0)
 AHEAD = 0
 RG = ("g", "g", "g", "s")
 HALO = "v"

@@ -17,7 +17,7 @@ FLOPS = 2 * 8 * 512 * 512 * 1536 + 2 * 8 * 1024 * 512 * 512
 
 MANUAL = True
 LAG = 6
-PLAN = (3, 0, 3, 0)
+PLAN = (2, 2, 2, 0)
 AHEAD = 0
 RG = ("g", "g", "g", "s")
 HALO = "v"
@@ -54,6 +54,7 @@ def tile_bilinearpairedlayer_pb_t_kernel(tc, t_bil, x_r, W_r, b_r, b_bil, out):
         br = sb.tile([P, 4], F32, name="br")
         bb_bf = sb.tile([P, 2], BF16, name="bb_bf")
         bbt = sb.tile([P, 512], F32, name="bbt")
+        bbf = sb.tile([P, 2], F32, name="bbf")
 
         pt = [ps.tile([P, 512], F32, name="pt%d" % i) for i in range(3)]
         p1 = [ps.tile([P, 512], F32, name="p1_%d" % i) for i in range(2)]
@@ -89,6 +90,7 @@ def tile_bilinearpairedlayer_pb_t_kernel(tc, t_bil, x_r, W_r, b_r, b_bil, out):
             nc.vector.memset(xg[i][:, 0:4], 0.0)
             nc.vector.memset(xg[i][:, 3068:3072], 0.0)
         nc.vector.tensor_copy(out=br[:], in_=br_bf[:])
+        nc.vector.tensor_copy(out=bbf[:], in_=bb_bf[:])
         nc.vector.tensor_copy(out=bbt[:].rearrange("p (j k) -> p j k", k=2),
                               in_=bb_bf[:].unsqueeze(1).to_broadcast([P, 256, 2]))
 
@@ -186,10 +188,16 @@ def tile_bilinearpairedlayer_pb_t_kernel(tc, t_bil, x_r, W_r, b_r, b_bil, out):
                                         rhs_scale=hs[b % 3][:, jh * 256:(jh + 1) * 256],
                                         start=True, stop=True)
                 c0 = (a % 2) * 1024 + jh * 512
-                nc.vector.tensor_tensor(out=o[:, c0:c0 + 512].rearrange("p (j k) -> p j k", k=2),
-                                        in0=bank[:].rearrange("p (k j) -> p j k", k=2),
-                                        in1=bbt[:].rearrange("p (j k) -> p j k", k=2),
-                                        op=ALU.add)
+                if a == 3 and jh == 1:
+                    for k in range(2):
+                        nc.scalar.activation(out=o[:, c0:c0 + 512].rearrange("p (j k) -> p j k", k=2)[:, :, k],
+                                             in_=bank[:, k * 256:(k + 1) * 256],
+                                             func=ACT.Identity, bias=bbf[:, k:k + 1], scale=1.0)
+                else:
+                    nc.vector.tensor_tensor(out=o[:, c0:c0 + 512].rearrange("p (j k) -> p j k", k=2),
+                                            in0=bank[:].rearrange("p (k j) -> p j k", k=2),
+                                            in1=bbt[:].rearrange("p (j k) -> p j k", k=2),
+                                            op=ALU.add)
             o_view = out[b].rearrange("(p a) j k -> p a (j k)", a=4)
             if b == B - 1:
                 nc.sync.dma_start(out=o_view[:, a, :], in_=o[:, (a % 2) * 1024:(a % 2 + 1) * 1024])

@@ -13,17 +13,14 @@ ALU = mybir.AluOpType
 
 P = 128
 B = 8
+BANK = 512
 FLOPS = 2 * 8 * 512 * 512 * 1536 + 2 * 8 * 1024 * 512 * 512
 
-MANUAL = True
+TICKS = 4
 LAG = 6
-PLAN = (2, 2, 2, 0)
-AHEAD = 0
-RG = ("g", "g", "g", "s")
-HALO = "v"
-QDELAY = 1
-QHQ = 0
-NT = 6
+FLIPS = (2, 2, 2, 0)
+T_TILES = 6
+GPSIMD_SHARE = 96
 
 
 def tile_bilinearpairedlayer_pb_t_kernel(tc, t_bil, x_r, W_r, b_r, b_bil, out):
@@ -33,47 +30,46 @@ def tile_bilinearpairedlayer_pb_t_kernel(tc, t_bil, x_r, W_r, b_r, b_bil, out):
         ps = ctx.enter_context(tc.psum_pool(name="ps", bufs=1))
 
         ident = sb.tile([P, P], F32, name="ident")
-        x_sb = [sb.tile([P, 2048], BF16, name="x%d" % i) for i in range(B)]
-        t_sb = [sb.tile([P, 4096], BF16, name="t%d" % i) for i in range(NT)]
-        w_sb = sb.tile([P, 6144], BF16, name="w_sb")
-        wg = sb.tile([P, 6144], BF16, name="wg", align_bytes=64)
-        wc = sb.tile([P, 1536], U32, name="wc", align_bytes=64)
-        ws = sb.tile([P, 1536], U8, name="ws", align_bytes=64)
-        xg = [sb.tile([P, 3072], BF16, name="xg%d" % i, align_bytes=64) for i in range(2)]
-        xc = [sb.tile([P, 768], U32, name="xc%d" % i, align_bytes=64) for i in range(3)]
-        xs = [sb.tile([P, 768], U8, name="xs%d" % i, align_bytes=64) for i in range(3)]
-        tg = [sb.tile([P, 2048], BF16, name="tg%d" % i, align_bytes=64) for i in range(4)]
-        tcd = [sb.tile([P, 1024], U32, name="tcd%d" % i, align_bytes=64) for i in range(3)]
-        tsc = [sb.tile([P, 1024], U8, name="tsc%d" % i, align_bytes=64) for i in range(3)]
-        hrt = [sb.tile([P, 2048], BF16, name="hrt%d" % i) for i in range(2)]
-        hg = [sb.tile([P, 2048], BF16, name="hg%d" % i, align_bytes=64) for i in range(2)]
-        hc = [sb.tile([P, 512], U32, name="hc%d" % i, align_bytes=64) for i in range(3)]
-        hs = [sb.tile([P, 512], U8, name="hs%d" % i, align_bytes=64) for i in range(3)]
-        o_sb = [sb.tile([P, 2048], F32, name="o%d" % i) for i in range(4)]
+        x_raw = [sb.tile([P, 2048], BF16, name="x_raw%d" % i) for i in range(B)]
+        t_raw = [sb.tile([P, 4096], BF16, name="t_raw%d" % i) for i in range(T_TILES)]
+        w_raw = sb.tile([P, 6144], BF16, name="w_raw")
+        w_lay = sb.tile([P, 6144], BF16, name="w_lay", align_bytes=64)
+        w_code = sb.tile([P, 1536], U32, name="w_code", align_bytes=64)
+        w_scale = sb.tile([P, 1536], U8, name="w_scale", align_bytes=64)
+        x_lay = [sb.tile([P, 3072], BF16, name="x_lay%d" % i, align_bytes=64) for i in range(2)]
+        x_code = [sb.tile([P, 768], U32, name="x_code%d" % i, align_bytes=64) for i in range(3)]
+        x_scale = [sb.tile([P, 768], U8, name="x_scale%d" % i, align_bytes=64) for i in range(3)]
+        t_lay = [sb.tile([P, 2048], BF16, name="t_lay%d" % i, align_bytes=64) for i in range(4)]
+        t_code = [sb.tile([P, 1024], U32, name="t_code%d" % i, align_bytes=64) for i in range(3)]
+        t_scale = [sb.tile([P, 1024], U8, name="t_scale%d" % i, align_bytes=64) for i in range(3)]
+        h_tiles = [sb.tile([P, 2048], BF16, name="h_tiles%d" % i) for i in range(2)]
+        h_lay = [sb.tile([P, 2048], BF16, name="h_lay%d" % i, align_bytes=64) for i in range(2)]
+        h_code = [sb.tile([P, 512], U32, name="h_code%d" % i, align_bytes=64) for i in range(3)]
+        h_scale = [sb.tile([P, 512], U8, name="h_scale%d" % i, align_bytes=64) for i in range(3)]
+        o_sb = [sb.tile([P, 2048], F32, name="o_sb%d" % i) for i in range(4)]
         br_bf = sb.tile([P, 4], BF16, name="br_bf")
         br = sb.tile([P, 4], F32, name="br")
         bb_bf = sb.tile([P, 2], BF16, name="bb_bf")
-        bbt = sb.tile([P, 512], F32, name="bbt")
-        bbf = sb.tile([P, 2], F32, name="bbf")
+        bb = sb.tile([P, 2], F32, name="bb")
+        bb_row = sb.tile([P, BANK], F32, name="bb_row")
+        warm = sb.tile([P, 2], F32, name="warm")
 
-        pt = [ps.tile([P, 512], F32, name="pt%d" % i) for i in range(3)]
-        p1 = [ps.tile([P, 512], F32, name="p1_%d" % i) for i in range(2)]
-        p2 = [ps.tile([P, 512], F32, name="p2_%d" % i) for i in range(3)]
-        cnt = {"pt": 0, "p1": 0, "p2": 0, "o": 0}
+        flip_bank = [ps.tile([P, BANK], F32, name="flip_bank%d" % i) for i in range(3)]
+        hid_bank = [ps.tile([P, BANK], F32, name="hid_bank%d" % i) for i in range(2)]
+        pair_bank = [ps.tile([P, BANK], F32, name="pair_bank%d" % i) for i in range(3)]
 
-        if MANUAL:
-            ctx.enter_context(tc.manual_schedule())
+        ctx.enter_context(tc.manual_schedule())
 
         def load_x(b):
-            nc.sync.dma_start(out=x_sb[b][:], in_=x_r[b].rearrange("(p a) f -> p (a f)", a=4))
+            nc.sync.dma_start(out=x_raw[b][:], in_=x_r[b].rearrange("(p a) f -> p (a f)", a=4))
 
         def load_t(b):
-            nc.sync.dma_start(out=t_sb[b % NT][:], in_=t_bil[b].rearrange("(p a) k g -> p (a k g)", a=4))
+            nc.sync.dma_start(out=t_raw[b % T_TILES][:], in_=t_bil[b].rearrange("(p a) k g -> p (a k g)", a=4))
 
-        w_view = W_r.rearrange("(u p e) f -> p u (e f)", u=2, e=2)
         load_x(0)
+        w_view = W_r.rearrange("(u p e) f -> p u (e f)", u=2, e=2)
         for u in range(2):
-            nc.sync.dma_start(out=w_sb[:, u * 3072:(u + 1) * 3072], in_=w_view[:, u, :])
+            nc.sync.dma_start(out=w_raw[:, u * 3072:(u + 1) * 3072], in_=w_view[:, u, :])
         with nc.allow_non_contiguous_dma(reason="two small bias vectors"):
             nc.scalar.dma_start(out=br_bf[:].rearrange("p (u e) -> p u e", u=2),
                                 in_=b_r.rearrange("(u p e) -> p u e", u=2, e=2))
@@ -82,161 +78,144 @@ def tile_bilinearpairedlayer_pb_t_kernel(tc, t_bil, x_r, W_r, b_r, b_bil, out):
         for b in range(B):
             if b + 2 < B:
                 load_x(b + 2)
-            if b < NT:
+            if b < T_TILES:
                 load_t(b)
 
+        nc.vector.memset(warm[:, 0:1], 0.0)
+        nc.scalar.activation(out=warm[:, 1:2], in_=warm[:, 0:1], func=ACT.Relu)
         masks.make_identity(nc, ident[:])
-        for i in range(2):
-            nc.vector.memset(xg[i][:, 0:4], 0.0)
-            nc.vector.memset(xg[i][:, 3068:3072], 0.0)
+        for lay in x_lay:
+            nc.vector.memset(lay[:, 0:4], 0.0)
+            nc.vector.memset(lay[:, 3068:3072], 0.0)
         nc.vector.tensor_copy(out=br[:], in_=br_bf[:])
-        nc.vector.tensor_copy(out=bbf[:], in_=bb_bf[:])
-        nc.vector.tensor_copy(out=bbt[:].rearrange("p (j k) -> p j k", k=2),
-                              in_=bb_bf[:].unsqueeze(1).to_broadcast([P, 256, 2]))
+        nc.vector.tensor_copy(out=bb[:], in_=bb_bf[:])
+        nc.vector.tensor_copy(out=bb_row[:].rearrange("p (j k) -> p j k", k=2),
+                              in_=bb_bf[:].unsqueeze(1).to_broadcast([P, BANK // 2, 2]))
 
-        def flip(src, m, dst, dst_off, eng):
-            bank = pt[cnt["pt"] % 3]
-            cnt["pt"] += 1
-            s32 = src[:].bitcast(F32)
+        def quantise(code, scale, first_word, lay, first_value, values):
+            words = slice(first_word, first_word + values // 4)
+            nc.vector.quantize_mx(out=code[:, words].bitcast(FP8X4), scales=scale[:, words],
+                                  in_=lay[:, first_value:first_value + values])
+
+        def flip(turn, raw, m, lay, first_word, copy):
+            bank = flip_bank[turn % 3]
+            words = raw[:].bitcast(F32)
             for i in range(4):
-                c0 = 512 * m + 128 * i
-                nc.tensor.transpose(bank[:, 128 * i:128 * (i + 1)], s32[:, c0:c0 + 128], ident[:])
-            o_ap = dst[:].bitcast(F32)[:, dst_off:dst_off + 512].rearrange("p (a c u) -> p a c u", a=2, u=2)
-            i_ap = bank[:].rearrange("p (a u c) -> p a c u", a=2, u=2)
-            if eng == "s":
-                nc.scalar.copy(out=o_ap, in_=i_ap)
-            else:
-                nc.vector.tensor_copy(out=o_ap, in_=i_ap)
+                nc.tensor.transpose(bank[:, P * i:P * (i + 1)], words[:, BANK * m + P * i:BANK * m + P * (i + 1)],
+                                    ident[:])
+            copy(out=lay[:].bitcast(F32)[:, first_word:first_word + BANK].rearrange("p (r c u) -> p r c u", r=2, u=2),
+                 in_=bank[:].rearrange("p (r u c) -> p r c u", r=2, u=2))
 
-        def quant(codes, scales, c_off, src, s_off, width):
-            nc.vector.quantize_mx(out=codes[:, c_off:c_off + width // 4].bitcast(FP8X4),
-                                  scales=scales[:, c_off:c_off + width // 4],
-                                  in_=src[:, s_off:s_off + width])
+        def flip_x(turn, b, m, copy):
+            flip(turn, x_raw[b], m, x_lay[b % 2], 256 + BANK * m, copy)
+            return [(quantise_x, b, 0)] if m == 1 else []
 
-        def copy_on(eng, o_ap, i_ap):
-            if eng == "v":
-                nc.vector.tensor_copy(out=o_ap, in_=i_ap)
-            elif eng == "s":
-                nc.scalar.copy(out=o_ap, in_=i_ap)
-            else:
-                nc.gpsimd.tensor_scalar(out=o_ap, in0=i_ap, scalar1=1.0, scalar2=0.0, op0=ALU.mult, op1=ALU.add)
+        def flip_w(turn, b, m, copy):
+            flip(turn, w_raw, m, w_lay, BANK * m, copy)
+            return [(quantise_w, b, m // 2)] if m % 2 == 1 else []
 
-        def job(kind, b, m, eng):
-            if kind == "x":
-                flip(x_sb[b], m, xg[b % 2], 256 + 512 * m, eng)
-                return [("x", b, 0)] if m == 1 else []
-            if kind == "w":
-                flip(w_sb, m, wg, 512 * m, eng)
-                return [("w", 0, m // 2)] if m % 2 == 1 else []
-            flip(t_sb[b % NT], m, tg[(2 * b + m // 2) % 4], 512 * (m % 2), eng)
-            if m == 3 and b + NT < B:
-                load_t(b + NT)
-            return [("t", b, m // 2)] if m % 2 == 1 else []
+        def flip_t(turn, b, m, copy):
+            flip(turn, t_raw[b % T_TILES], m, t_lay[(2 * b + m // 2) % 4], BANK * (m % 2), copy)
+            if m == 3 and b + T_TILES < B:
+                load_t(b + T_TILES)
+            return [(quantise_t, b, m // 2)] if m % 2 == 1 else []
 
-        def quantise(kind, b, h):
-            if kind == "x":
-                g = xg[b % 2]
-                copy_on(HALO, g[:, 2560:3068], g[:, 516:1024])
-                copy_on(HALO, g[:, 4:512], g[:, 2048:2556])
-                quant(xc[b % 3], xs[b % 3], 0, g, 0, 2048)
-                quant(xc[b % 3], xs[b % 3], 512, g, 2048, 1024)
-            elif kind == "w":
-                quant(wc, ws, 512 * h, wg, 2048 * h, 2048)
-            else:
-                quant(tcd[b % 3], tsc[b % 3], 512 * h, tg[(2 * b + h) % 4], 0, 2048)
+        def quantise_x(b, half):
+            lay = x_lay[b % 2]
+            nc.vector.tensor_copy(out=lay[:, 2560:3068], in_=lay[:, 516:1024])
+            nc.vector.tensor_copy(out=lay[:, 4:512], in_=lay[:, 2048:2556])
+            quantise(x_code[b % 3], x_scale[b % 3], 0, lay, 0, 2048)
+            quantise(x_code[b % 3], x_scale[b % 3], 512, lay, 2048, 1024)
 
-        def s1(b, t):
-            bank = p1[cnt["p1"] % 2]
-            cnt["p1"] += 1
-            for w, off in ((0, 128), (1, 256), (2, 0)):
-                s = t * 3 + w
+        def quantise_w(b, third):
+            quantise(w_code, w_scale, 512 * third, w_lay, 2048 * third, 2048)
+
+        def quantise_t(b, half):
+            quantise(t_code[b % 3], t_scale[b % 3], 512 * half, t_lay[(2 * b + half) % 4], 0, 2048)
+
+        def hidden_tile(b, t):
+            bank = hid_bank[t % 2]
+            for w, first in ((0, 128), (1, 256), (2, 0)):
+                cols = slice((3 * t + w) * P, (3 * t + w + 1) * P)
                 nc.tensor.matmul_mx(out=bank[:],
-                                    lhsT=wc[:, s * 128:(s + 1) * 128].bitcast(FP8X4),
-                                    lhsT_scale=ws[:, s * 128:(s + 1) * 128],
-                                    rhs=xc[b % 3][:, off:off + 512].bitcast(FP8X4),
-                                    rhs_scale=xs[b % 3][:, off:off + 512],
+                                    lhsT=w_code[:, cols].bitcast(FP8X4), lhsT_scale=w_scale[:, cols],
+                                    rhs=x_code[b % 3][:, first:first + BANK].bitcast(FP8X4),
+                                    rhs_scale=x_scale[b % 3][:, first:first + BANK],
                                     start=(w == 0), stop=(w == 2))
-            nc.scalar.activation(out=hrt[b % 2][:, t * 512:(t + 1) * 512].rearrange("p (q a) -> p q a", a=4),
+            nc.scalar.activation(out=h_tiles[b % 2][:, t * BANK:(t + 1) * BANK].rearrange("p (q a) -> p q a", a=4),
                                  in_=bank[:].rearrange("p (a q) -> p q a", a=4),
                                  func=ACT.Relu, bias=br[:, t:t + 1], scale=1.0)
 
         def regroup(b):
-            n = len(RG)
-            dst = hg[b % 2][:].rearrange("p (c i t) -> p c t i", i=4, t=4)
-            src = hrt[b % 2][:].rearrange("p (t c i) -> p c t i", t=4, i=4)
-            for i in range(n):
-                c0 = 128 * i // n
-                c1 = 128 * (i + 1) // n
-                copy_on(RG[i], dst[:, c0:c1], src[:, c0:c1])
+            lay = h_lay[b % 2][:].rearrange("p (c i t) -> p c t i", i=4, t=4)
+            tiles = h_tiles[b % 2][:].rearrange("p (t c i) -> p c t i", t=4, i=4)
+            nc.gpsimd.tensor_scalar(out=lay[:, 0:GPSIMD_SHARE], in0=tiles[:, 0:GPSIMD_SHARE],
+                                    scalar1=1.0, scalar2=0.0, op0=ALU.mult, op1=ALU.add)
+            nc.scalar.copy(out=lay[:, GPSIMD_SHARE:P], in_=tiles[:, GPSIMD_SHARE:P])
 
-        def qh(b):
-            quant(hc[b % 3], hs[b % 3], 0, hg[b % 2], 0, 2048)
+        def quantise_h(b):
+            quantise(h_code[b % 3], h_scale[b % 3], 0, h_lay[b % 2], 0, 2048)
 
-        def s2(b, a):
-            if a % 2 == 0:
-                cnt["o"] += 1
-            o = o_sb[(cnt["o"] - 1) % 4]
-            for jh in range(2):
-                bank = p2[cnt["p2"] % 3]
-                cnt["p2"] += 1
+        def pair_block(b, a):
+            o = o_sb[(2 * b + a // 2) % 4]
+            for half in range(2):
+                bank = pair_bank[(8 * b + 2 * a + half) % 3]
+                js = slice(half * 256, (half + 1) * 256)
                 for k in range(2):
-                    s = 2 * a + k
+                    cols = slice((2 * a + k) * P, (2 * a + k + 1) * P)
                     nc.tensor.matmul_mx(out=bank[:, k * 256:(k + 1) * 256],
-                                        lhsT=tcd[b % 3][:, s * 128:(s + 1) * 128].bitcast(FP8X4),
-                                        lhsT_scale=tsc[b % 3][:, s * 128:(s + 1) * 128],
-                                        rhs=hc[b % 3][:, jh * 256:(jh + 1) * 256].bitcast(FP8X4),
-                                        rhs_scale=hs[b % 3][:, jh * 256:(jh + 1) * 256],
+                                        lhsT=t_code[b % 3][:, cols].bitcast(FP8X4), lhsT_scale=t_scale[b % 3][:, cols],
+                                        rhs=h_code[b % 3][:, js].bitcast(FP8X4), rhs_scale=h_scale[b % 3][:, js],
                                         start=True, stop=True)
-                c0 = (a % 2) * 1024 + jh * 512
-                if a == 3 and jh == 1:
+                first = (a % 2) * 1024 + half * BANK
+                o_jk = o[:, first:first + BANK].rearrange("p (j k) -> p j k", k=2)
+                if a == 3 and half == 1:
                     for k in range(2):
-                        nc.scalar.activation(out=o[:, c0:c0 + 512].rearrange("p (j k) -> p j k", k=2)[:, :, k],
-                                             in_=bank[:, k * 256:(k + 1) * 256],
-                                             func=ACT.Identity, bias=bbf[:, k:k + 1], scale=1.0)
+                        nc.scalar.activation(out=o_jk[:, :, k], in_=bank[:, k * 256:(k + 1) * 256],
+                                             func=ACT.Identity, bias=bb[:, k:k + 1], scale=1.0)
                 else:
-                    nc.vector.tensor_tensor(out=o[:, c0:c0 + 512].rearrange("p (j k) -> p j k", k=2),
-                                            in0=bank[:].rearrange("p (k j) -> p j k", k=2),
-                                            in1=bbt[:].rearrange("p (j k) -> p j k", k=2),
-                                            op=ALU.add)
-            o_view = out[b].rearrange("(p a) j k -> p a (j k)", a=4)
+                    nc.vector.tensor_tensor(out=o_jk, in0=bank[:].rearrange("p (k j) -> p j k", k=2),
+                                            in1=bb_row[:].rearrange("p (j k) -> p j k", k=2), op=ALU.add)
+            rows = out[b].rearrange("(p a) j k -> p a (j k)", a=4)
             if b == B - 1:
-                nc.sync.dma_start(out=o_view[:, a, :], in_=o[:, (a % 2) * 1024:(a % 2 + 1) * 1024])
+                nc.sync.dma_start(out=rows[:, a, :], in_=o[:, (a % 2) * 1024:(a % 2 + 1) * 1024])
             elif a % 2 == 1:
-                nc.sync.dma_start(out=o_view[:, a - 1:a + 1, :], in_=o[:].rearrange("p (a r) -> p a r", a=2))
+                nc.sync.dma_start(out=rows[:, a - 1:a + 1, :], in_=o[:].rearrange("p (a r) -> p a r", a=2))
 
-        jobs = [("x", 0, 0), ("x", 0, 1)] + [("w", 0, m) for m in range(6)] + [("x", 1, 0), ("x", 1, 1)]
+        flips = [(flip_x, 0, 0), (flip_x, 0, 1)] + [(flip_w, 0, m) for m in range(6)] + [(flip_x, 1, 0), (flip_x, 1, 1)]
         for b in range(B):
             if b + 2 < B:
-                jobs += [("x", b + 2, 0), ("x", b + 2, 1)]
-            jobs += [("t", b, m) for m in range(4)]
-        todo = []
-        for i in range(8 + AHEAD):
-            ready = todo
-            kind, b, m = jobs[i]
-            todo = job(kind, b, m, "v" if i % 2 else "s")
-            for kind, b, h in ready:
-                quantise(kind, b, h)
-        for kind, b, h in todo:
-            quantise(kind, b, h)
-        nxt = 8 + AHEAD
-        waiting = []
-        for tick in range(4 * B + LAG):
-            n = tick // 4
-            q = tick % 4
+                flips += [(flip_x, b + 2, 0), (flip_x, b + 2, 1)]
+            flips += [(flip_t, b, m) for m in range(4)]
+
+        start = 8
+        steps = []
+        for turn in range(start):
+            ready = steps
+            fn, b, m = flips[turn]
+            steps = fn(turn, b, m, nc.vector.tensor_copy if turn % 2 else nc.scalar.copy)
+            for fn, b, part in ready:
+                fn(b, part)
+        for fn, b, part in steps:
+            fn(b, part)
+
+        turn = start
+        steps = []
+        for tick in range(TICKS * B + LAG):
+            n = tick // TICKS
+            q = tick % TICKS
+            ready = steps
+            steps = []
             if q == 0 and 1 <= n <= B:
                 regroup(n - 1)
-            for i in range(PLAN[q]):
-                if nxt < len(jobs):
-                    kind, b, m = jobs[nxt]
-                    nxt += 1
-                    waiting += [(tick + QDELAY, item) for item in job(kind, b, m, "s")]
+            for fn, b, m in flips[turn:turn + FLIPS[q]]:
+                steps += fn(turn, b, m, nc.scalar.copy)
+                turn += 1
             if n < B:
-                s1(n, q)
+                hidden_tile(n, q)
             if tick >= LAG:
-                s2((tick - LAG) // 4, (tick - LAG) % 4)
-            if q == QHQ and 1 <= n <= B:
-                qh(n - 1)
-            for due, item in waiting:
-                if due <= tick:
-                    quantise(item[0], item[1], item[2])
-            waiting = [(due, item) for due, item in waiting if due > tick]
+                pair_block((tick - LAG) // TICKS, (tick - LAG) % TICKS)
+            if q == 0 and 1 <= n <= B:
+                quantise_h(n - 1)
+            for fn, b, part in ready:
+                fn(b, part)

from contextlib import ExitStack

import concourse.masks as masks
import concourse.mybir as mybir

F32 = mybir.dt.float32
BF16 = mybir.dt.bfloat16
U32 = mybir.dt.uint32
U8 = mybir.dt.uint8
FP8X4 = mybir.dt.float8_e4m3fn_x4
ACT = mybir.ActivationFunctionType
ALU = mybir.AluOpType

P = 128
B = 8
BANK = 512
FLOPS = 2 * 8 * 512 * 512 * 1536 + 2 * 8 * 1024 * 512 * 512

TICKS = 4
LAG = 6
FLIPS = (2, 2, 2, 0)
T_TILES = 6
GPSIMD_SHARE = 96


def tile_bilinearpairedlayer_pb_t_kernel(tc, t_bil, x_r, W_r, b_r, b_bil, out):
    nc = tc.nc
    with ExitStack() as ctx:
        sb = ctx.enter_context(tc.tile_pool(name="sb", bufs=1))
        ps = ctx.enter_context(tc.psum_pool(name="ps", bufs=1))

        ident = sb.tile([P, P], F32, name="ident")
        x_raw = [sb.tile([P, 2048], BF16, name="x_raw%d" % i) for i in range(B)]
        t_raw = [sb.tile([P, 4096], BF16, name="t_raw%d" % i) for i in range(T_TILES)]
        w_raw = sb.tile([P, 6144], BF16, name="w_raw")
        w_lay = sb.tile([P, 6144], BF16, name="w_lay", align_bytes=64)
        w_code = sb.tile([P, 1536], U32, name="w_code", align_bytes=64)
        w_scale = sb.tile([P, 1536], U8, name="w_scale", align_bytes=64)
        x_lay = [sb.tile([P, 3072], BF16, name="x_lay%d" % i, align_bytes=64) for i in range(2)]
        x_code = [sb.tile([P, 768], U32, name="x_code%d" % i, align_bytes=64) for i in range(3)]
        x_scale = [sb.tile([P, 768], U8, name="x_scale%d" % i, align_bytes=64) for i in range(3)]
        t_lay = [sb.tile([P, 2048], BF16, name="t_lay%d" % i, align_bytes=64) for i in range(4)]
        t_code = [sb.tile([P, 1024], U32, name="t_code%d" % i, align_bytes=64) for i in range(3)]
        t_scale = [sb.tile([P, 1024], U8, name="t_scale%d" % i, align_bytes=64) for i in range(3)]
        h_tiles = [sb.tile([P, 2048], BF16, name="h_tiles%d" % i) for i in range(2)]
        h_lay = [sb.tile([P, 2048], BF16, name="h_lay%d" % i, align_bytes=64) for i in range(2)]
        h_code = [sb.tile([P, 512], U32, name="h_code%d" % i, align_bytes=64) for i in range(3)]
        h_scale = [sb.tile([P, 512], U8, name="h_scale%d" % i, align_bytes=64) for i in range(3)]
        o_sb = [sb.tile([P, 2048], F32, name="o_sb%d" % i) for i in range(4)]
        br_bf = sb.tile([P, 4], BF16, name="br_bf")
        br = sb.tile([P, 4], F32, name="br")
        bb_bf = sb.tile([P, 2], BF16, name="bb_bf")
        bb = sb.tile([P, 2], F32, name="bb")
        bb_row = sb.tile([P, BANK], F32, name="bb_row")
        warm = sb.tile([P, 2], F32, name="warm")

        flip_bank = [ps.tile([P, BANK], F32, name="flip_bank%d" % i) for i in range(3)]
        hid_bank = [ps.tile([P, BANK], F32, name="hid_bank%d" % i) for i in range(2)]
        pair_bank = [ps.tile([P, BANK], F32, name="pair_bank%d" % i) for i in range(3)]

        ctx.enter_context(tc.manual_schedule())

        def load_x(b):
            nc.sync.dma_start(out=x_raw[b][:], in_=x_r[b].rearrange("(p a) f -> p (a f)", a=4))

        def load_t(b):
            nc.sync.dma_start(out=t_raw[b % T_TILES][:], in_=t_bil[b].rearrange("(p a) k g -> p (a k g)", a=4))

        load_x(0)
        w_view = W_r.rearrange("(u p e) f -> p u (e f)", u=2, e=2)
        for u in range(2):
            nc.sync.dma_start(out=w_raw[:, u * 3072:(u + 1) * 3072], in_=w_view[:, u, :])
        with nc.allow_non_contiguous_dma(reason="two small bias vectors"):
            nc.scalar.dma_start(out=br_bf[:].rearrange("p (u e) -> p u e", u=2),
                                in_=b_r.rearrange("(u p e) -> p u e", u=2, e=2))
            nc.scalar.dma_start(out=bb_bf[:], in_=b_bil.partition_broadcast(P))
        load_x(1)
        for b in range(B):
            if b + 2 < B:
                load_x(b + 2)
            if b < T_TILES:
                load_t(b)

        nc.vector.memset(warm[:, 0:1], 0.0)
        nc.scalar.activation(out=warm[:, 1:2], in_=warm[:, 0:1], func=ACT.Relu)
        masks.make_identity(nc, ident[:])
        for lay in x_lay:
            nc.vector.memset(lay[:, 0:4], 0.0)
            nc.vector.memset(lay[:, 3068:3072], 0.0)
        nc.vector.tensor_copy(out=br[:], in_=br_bf[:])
        nc.vector.tensor_copy(out=bb[:], in_=bb_bf[:])
        nc.vector.tensor_copy(out=bb_row[:].rearrange("p (j k) -> p j k", k=2),
                              in_=bb_bf[:].unsqueeze(1).to_broadcast([P, BANK // 2, 2]))

        def quantise(code, scale, first_word, lay, first_value, values):
            words = slice(first_word, first_word + values // 4)
            nc.vector.quantize_mx(out=code[:, words].bitcast(FP8X4), scales=scale[:, words],
                                  in_=lay[:, first_value:first_value + values])

        def flip(turn, raw, m, lay, first_word, copy):
            bank = flip_bank[turn % 3]
            words = raw[:].bitcast(F32)
            for i in range(4):
                nc.tensor.transpose(bank[:, P * i:P * (i + 1)], words[:, BANK * m + P * i:BANK * m + P * (i + 1)],
                                    ident[:])
            copy(out=lay[:].bitcast(F32)[:, first_word:first_word + BANK].rearrange("p (r c u) -> p r c u", r=2, u=2),
                 in_=bank[:].rearrange("p (r u c) -> p r c u", r=2, u=2))

        def flip_x(turn, b, m, copy):
            flip(turn, x_raw[b], m, x_lay[b % 2], 256 + BANK * m, copy)
            return [(quantise_x, b, 0)] if m == 1 else []

        def flip_w(turn, b, m, copy):
            flip(turn, w_raw, m, w_lay, BANK * m, copy)
            return [(quantise_w, b, m // 2)] if m % 2 == 1 else []

        def flip_t(turn, b, m, copy):
            flip(turn, t_raw[b % T_TILES], m, t_lay[(2 * b + m // 2) % 4], BANK * (m % 2), copy)
            if m == 3 and b + T_TILES < B:
                load_t(b + T_TILES)
            return [(quantise_t, b, m // 2)] if m % 2 == 1 else []

        def quantise_x(b, half):
            lay = x_lay[b % 2]
            nc.vector.tensor_copy(out=lay[:, 2560:3068], in_=lay[:, 516:1024])
            nc.vector.tensor_copy(out=lay[:, 4:512], in_=lay[:, 2048:2556])
            quantise(x_code[b % 3], x_scale[b % 3], 0, lay, 0, 2048)
            quantise(x_code[b % 3], x_scale[b % 3], 512, lay, 2048, 1024)

        def quantise_w(b, third):
            quantise(w_code, w_scale, 512 * third, w_lay, 2048 * third, 2048)

        def quantise_t(b, half):
            quantise(t_code[b % 3], t_scale[b % 3], 512 * half, t_lay[(2 * b + half) % 4], 0, 2048)

        def hidden_tile(b, t):
            bank = hid_bank[t % 2]
            for w, first in ((0, 128), (1, 256), (2, 0)):
                cols = slice((3 * t + w) * P, (3 * t + w + 1) * P)
                nc.tensor.matmul_mx(out=bank[:],
                                    lhsT=w_code[:, cols].bitcast(FP8X4), lhsT_scale=w_scale[:, cols],
                                    rhs=x_code[b % 3][:, first:first + BANK].bitcast(FP8X4),
                                    rhs_scale=x_scale[b % 3][:, first:first + BANK],
                                    start=(w == 0), stop=(w == 2))
            nc.scalar.activation(out=h_tiles[b % 2][:, t * BANK:(t + 1) * BANK].rearrange("p (q a) -> p q a", a=4),
                                 in_=bank[:].rearrange("p (a q) -> p q a", a=4),
                                 func=ACT.Relu, bias=br[:, t:t + 1], scale=1.0)

        def regroup(b):
            lay = h_lay[b % 2][:].rearrange("p (c i t) -> p c t i", i=4, t=4)
            tiles = h_tiles[b % 2][:].rearrange("p (t c i) -> p c t i", t=4, i=4)
            nc.gpsimd.tensor_scalar(out=lay[:, 0:GPSIMD_SHARE], in0=tiles[:, 0:GPSIMD_SHARE],
                                    scalar1=1.0, scalar2=0.0, op0=ALU.mult, op1=ALU.add)
            nc.scalar.copy(out=lay[:, GPSIMD_SHARE:P], in_=tiles[:, GPSIMD_SHARE:P])

        def quantise_h(b):
            quantise(h_code[b % 3], h_scale[b % 3], 0, h_lay[b % 2], 0, 2048)

        def pair_block(b, a):
            o = o_sb[(2 * b + a // 2) % 4]
            for half in range(2):
                bank = pair_bank[(8 * b + 2 * a + half) % 3]
                js = slice(half * 256, (half + 1) * 256)
                for k in range(2):
                    cols = slice((2 * a + k) * P, (2 * a + k + 1) * P)
                    nc.tensor.matmul_mx(out=bank[:, k * 256:(k + 1) * 256],
                                        lhsT=t_code[b % 3][:, cols].bitcast(FP8X4), lhsT_scale=t_scale[b % 3][:, cols],
                                        rhs=h_code[b % 3][:, js].bitcast(FP8X4), rhs_scale=h_scale[b % 3][:, js],
                                        start=True, stop=True)
                first = (a % 2) * 1024 + half * BANK
                o_jk = o[:, first:first + BANK].rearrange("p (j k) -> p j k", k=2)
                if a == 3 and half == 1:
                    for k in range(2):
                        nc.scalar.activation(out=o_jk[:, :, k], in_=bank[:, k * 256:(k + 1) * 256],
                                             func=ACT.Identity, bias=bb[:, k:k + 1], scale=1.0)
                else:
                    nc.vector.tensor_tensor(out=o_jk, in0=bank[:].rearrange("p (k j) -> p j k", k=2),
                                            in1=bb_row[:].rearrange("p (j k) -> p j k", k=2), op=ALU.add)
            rows = out[b].rearrange("(p a) j k -> p a (j k)", a=4)
            if b == B - 1:
                nc.sync.dma_start(out=rows[:, a, :], in_=o[:, (a % 2) * 1024:(a % 2 + 1) * 1024])
            elif a % 2 == 1:
                nc.sync.dma_start(out=rows[:, a - 1:a + 1, :], in_=o[:].rearrange("p (a r) -> p a r", a=2))

        flips = [(flip_x, 0, 0), (flip_x, 0, 1)] + [(flip_w, 0, m) for m in range(6)] + [(flip_x, 1, 0), (flip_x, 1, 1)]
        for b in range(B):
            if b + 2 < B:
                flips += [(flip_x, b + 2, 0), (flip_x, b + 2, 1)]
            flips += [(flip_t, b, m) for m in range(4)]

        start = 8
        steps = []
        for turn in range(start):
            ready = steps
            fn, b, m = flips[turn]
            steps = fn(turn, b, m, nc.vector.tensor_copy if turn % 2 else nc.scalar.copy)
            for fn, b, part in ready:
                fn(b, part)
        for fn, b, part in steps:
            fn(b, part)

        turn = start
        steps = []
        for tick in range(TICKS * B + LAG):
            n = tick // TICKS
            q = tick % TICKS
            ready = steps
            steps = []
            if q == 0 and 1 <= n <= B:
                regroup(n - 1)
            for fn, b, m in flips[turn:turn + FLIPS[q]]:
                steps += fn(turn, b, m, nc.scalar.copy)
                turn += 1
            if n < B:
                hidden_tile(n, q)
            if tick >= LAG:
                pair_block((tick - LAG) // TICKS, (tick - LAG) % TICKS)
            if q == 0 and 1 <= n <= B:
                quantise_h(n - 1)
            for fn, b, part in ready:
                fn(b, part)
